import numpy as np
import ml_dtypes


def mxq(x, axis, fmt="e4m3"):
    dtype, down = {"e4m3": (ml_dtypes.float8_e4m3fn, 7), "e5m2": (ml_dtypes.float8_e5m2, 14)}[fmt]
    v = np.moveaxis(np.asarray(x, np.float32).astype(ml_dtypes.bfloat16).astype(np.float64), axis, -1)
    blocks = v.reshape(v.shape[:-1] + (-1, 32))
    amax = np.abs(blocks).max(-1, keepdims=True)
    byte = np.maximum(np.where(amax > 0, np.frexp(amax)[1] - 1 + 127, 0) - down, 1)
    scale = np.exp2(byte - 127.0)
    codes = (blocks / scale).astype(np.float32).astype(dtype).astype(np.float64)
    return np.moveaxis((codes * scale).reshape(v.shape), -1, axis)


WIDE = False


def mx_kscale(k):
    if not WIDE:
        return np.ones(k)
    levels = np.array([10, -10, 5, -5, 0])
    if k % 512:
        return np.exp2(np.random.permutation(np.resize(levels, k // 32))).repeat(32)
    a = np.empty((k // 512, 16))
    for p in range(k // 512):
        a[p, :8] = np.random.permutation(np.resize(levels, 8))
        for g in range(8):
            far = levels[np.abs(levels - a[p, g]) >= 10]
            a[p, g + 8] = far[np.random.randint(len(far))]
    return np.exp2(a.ravel()).repeat(32)


BF16 = ml_dtypes.bfloat16


def bf(x):
    return np.asarray(x, np.float32).astype(BF16)


def f64(x):
    return np.asarray(x).astype(np.float64)


B, N, D, H, DK, DV = 4, 4096, 512, 4, 64, 64


def xnorm(x, g):
    n = np.sqrt(np.sum(x * x, axis=-1, keepdims=True))
    return x * g / n


def setup_inputs():
    s = mx_kscale(D)
    return {
        "queries": bf(np.random.standard_normal((B, N, D)) * s),
        "Wq": bf(np.random.standard_normal((D, H * DK)) / np.sqrt(D) / s[:, None]),
        "bq": bf(np.random.standard_normal(H * DK) * 0.1),
        "gamma": bf(np.random.standard_normal((1, H, 1, 1)) * 2.0),
    }


def reference(queries, Wq, bq, gamma):
    q = ((mxq(f64(queries), 2, "e4m3") @ mxq(f64(Wq), 0, "e4m3")) + f64(bq)).reshape(B, N, H, DK)
    return xnorm(q.transpose(0, 2, 1, 3), f64(gamma))

@@ -1,0 +1,238 @@
+from contextlib import ExitStack
+
+import concourse.mybir as mybir
+from concourse.masks import make_identity
+
+F32 = mybir.dt.float32
+BF16 = mybir.dt.bfloat16
+U32 = mybir.dt.uint32
+U8 = mybir.dt.uint8
+FP8X4 = mybir.dt.float8_e4m3fn_x4
+ACT = mybir.ActivationFunctionType
+ALU = mybir.AluOpType
+
+P = 128
+BATCH, TOKENS, K = 4, 4096, 512
+HEADS, HEAD_DIM = 4, 64
+OUT_COLS = HEADS * HEAD_DIM
+PACK = 4
+WORDS = K // 2
+
+ROUND_TILES = 4
+ROUND_TOKENS = P * ROUND_TILES
+ROUNDS_PER_BATCH = TOKENS // ROUND_TOKENS
+ROUNDS = BATCH * ROUNDS_PER_BATCH
+BANK_TILES = 2
+BANKS = ROUND_TILES // BANK_TILES
+LOAD_AHEAD = 6
+GPSIMD_TILES = 3
+
+FLOPS = 2 * BATCH * TOKENS * K * OUT_COLS
+
+
+def tile_ufoattention_pb_t_kernel(tc, queries, Wq, bq, gamma, out):
+    nc = tc.nc
+    with ExitStack() as ctx:
+        ctx.enter_context(tc.manual_schedule())
+        const = ctx.enter_context(tc.tile_pool(name="const", bufs=1))
+        x_pool = ctx.enter_context(tc.tile_pool(name="x", bufs=LOAD_AHEAD + 2))
+        mx_pool = ctx.enter_context(tc.tile_pool(name="mx", bufs=3))
+        q_pool = ctx.enter_context(tc.tile_pool(name="q", bufs=8))
+        small = ctx.enter_context(tc.tile_pool(name="small", bufs=10))
+        sq_pool = ctx.enter_context(tc.tile_pool(name="sq", bufs=3))
+        psum_t = ctx.enter_context(tc.psum_pool(name="psum_t", bufs=2 * BANKS))
+        psum_q = ctx.enter_context(tc.psum_pool(name="psum_q", bufs=2 * BANKS))
+
+        x_rounds = queries.flatten_outer_dims().rearrange(
+            "(r p i) k -> r p (i k)", p=P, i=ROUND_TILES
+        )
+
+        x_tiles, xt_banks, grouped_tiles, code_tiles, scale_tiles = {}, {}, {}, {}, {}
+        acc_banks, q_tiles, square_tiles, sumsq_tiles, rnorm_tiles, gain_tiles = {}, {}, {}, {}, {}, {}
+
+        def load(r):
+            x_tiles[r] = x_pool.tile([P, ROUND_TILES * K], BF16, name="x_sb")
+            nc.sync.dma_start(out=x_tiles[r][:], in_=x_rounds[r])
+
+        for r in range(LOAD_AHEAD):
+            load(r)
+
+        ident = const.tile([P, P], F32)
+        make_identity(nc, ident[:])
+
+        w_raw = const.tile([P, PACK, OUT_COLS], BF16)
+        nc.scalar.dma_start(
+            out=w_raw[:],
+            in_=Wq.rearrange("(p t) c -> p t c", t=PACK),
+        )
+        bias_bf = const.tile([P, OUT_COLS], BF16)
+        nc.scalar.dma_start(out=bias_bf[:], in_=bq.partition_broadcast(P))
+        gamma_bf = const.tile([P, HEADS], BF16)
+        nc.scalar.dma_start(
+            out=gamma_bf[:],
+            in_=gamma.rearrange("a h b c -> (a h b c)").partition_broadcast(P),
+        )
+
+        one = const.tile([P, 1], F32)
+        nc.vector.memset(one[:], 1.0)
+        nc.scalar.activation(out=one[:], in_=one[:], func=ACT.Abs_reciprocal_sqrt)
+
+        w_grouped = const.tile([P, OUT_COLS, PACK], BF16, align_bytes=64)
+        nc.vector.tensor_copy(out=w_grouped[:], in_=w_raw[:].rearrange("p t c -> p c t"))
+        w_codes = const.tile([P, OUT_COLS], U32, align_bytes=64)
+        w_scales = const.tile([P, OUT_COLS], U8, align_bytes=64)
+        nc.vector.quantize_mx(
+            out=w_codes[:].bitcast(FP8X4),
+            scales=w_scales[:],
+            in_=w_grouped[:].rearrange("p c t -> p (c t)"),
+        )
+        bias_bank = const.tile([P, HEADS, BANK_TILES, HEAD_DIM], F32)
+        for i in range(BANK_TILES):
+            nc.vector.tensor_copy(
+                out=bias_bank[:, :, i, :],
+                in_=bias_bf[:].rearrange("p (h d) -> p h d", h=HEADS),
+            )
+        gamma_round = const.tile([P, HEADS, ROUND_TILES], F32)
+        nc.vector.tensor_copy(
+            out=gamma_round[:],
+            in_=gamma_bf[:].unsqueeze(2).to_broadcast([P, HEADS, ROUND_TILES]),
+        )
+
+        def transpose(r):
+            x_words = x_tiles[r][:].bitcast(F32)
+            xt_banks[r] = []
+            for bank in range(BANKS):
+                xt = psum_t.tile([P, BANK_TILES, 2, P], F32, name="xt")
+                for i in range(BANK_TILES):
+                    for u in range(2):
+                        first = (bank * BANK_TILES + i) * WORDS
+                        nc.tensor.transpose(
+                            xt[:, i, u, :], x_words[:, first + u : first + WORDS : 2], ident[:]
+                        )
+                xt_banks[r].append(xt)
+
+        def regroup(r):
+            grouped_tiles[r] = mx_pool.tile([P, ROUND_TILES * K], BF16, align_bytes=64, name="grouped")
+            grouped_words = grouped_tiles[r][:].bitcast(F32)
+            for bank, xt in enumerate(xt_banks[r]):
+                dst = grouped_words[
+                    :, bank * BANK_TILES * WORDS : (bank + 1) * BANK_TILES * WORDS
+                ].rearrange("p (i r u) -> p i r u", i=BANK_TILES, u=2)
+                src = xt[:].rearrange("p i u r -> p i r u")
+                nc.scalar.copy(out=dst, in_=src)
+
+        def quantise(r):
+            code_tiles[r] = mx_pool.tile([P, ROUND_TILES * P], U32, align_bytes=64, name="codes")
+            scale_tiles[r] = mx_pool.tile([P, ROUND_TILES * P], U8, align_bytes=64, name="scales")
+            nc.vector.quantize_mx(
+                out=code_tiles[r][:].bitcast(FP8X4),
+                scales=scale_tiles[r][:],
+                in_=grouped_tiles[r][:],
+            )
+
+        def project(r):
+            codes, scales = code_tiles[r], scale_tiles[r]
+            acc_banks[r] = []
+            for bank in range(BANKS):
+                acc = psum_q.tile([P, BANK_TILES, OUT_COLS], F32, name="acc")
+                for i in range(BANK_TILES):
+                    cols = slice((bank * BANK_TILES + i) * P, (bank * BANK_TILES + i + 1) * P)
+                    nc.tensor.matmul_mx(
+                        out=acc[:, i, :],
+                        lhsT=codes[:, cols].bitcast(FP8X4),
+                        lhsT_scale=scales[:, cols],
+                        rhs=w_codes[:].bitcast(FP8X4),
+                        rhs_scale=w_scales[:],
+                        start=True,
+                        stop=True,
+                    )
+                acc_banks[r].append(acc)
+
+        def add_bias(r):
+            q_tiles[r] = q_pool.tile([P, HEADS, ROUND_TILES, HEAD_DIM], F32, name="q_sb")
+            q_round = q_tiles[r]
+            for bank, acc in enumerate(acc_banks[r]):
+                nc.vector.tensor_tensor(
+                    out=q_round[:, :, bank * BANK_TILES : (bank + 1) * BANK_TILES, :],
+                    in0=acc[:].rearrange("p i (h d) -> p h i d", h=HEADS),
+                    in1=bias_bank[:],
+                    op=ALU.add,
+                )
+
+        def square(r):
+            square_tiles[r] = sq_pool.tile([P, HEADS, ROUND_TILES, HEAD_DIM], F32, name="squares")
+            nc.scalar.activation(out=square_tiles[r][:], in_=q_tiles[r][:], func=ACT.Square)
+
+        def sum_squares(r):
+            sumsq_tiles[r] = small.tile([P, HEADS, ROUND_TILES], F32, name="sumsq")
+            nc.vector.tensor_reduce(
+                out=sumsq_tiles[r][:], in_=square_tiles[r][:], axis=mybir.AxisListType.X, op=ALU.add
+            )
+
+        def reciprocal_norm(r):
+            rnorm_tiles[r] = small.tile([P, HEADS, ROUND_TILES], F32, name="rnorm")
+            nc.scalar.activation(
+                out=rnorm_tiles[r][:], in_=sumsq_tiles[r][:], func=ACT.Abs_reciprocal_sqrt
+            )
+
+        def gains(r):
+            gain_tiles[r] = small.tile([P, HEADS, ROUND_TILES], F32, name="gain")
+            nc.vector.tensor_tensor(
+                out=gain_tiles[r][:], in0=rnorm_tiles[r][:], in1=gamma_round[:], op=ALU.mult
+            )
+
+        def scale(r):
+            q_round, gain = q_tiles[r], gain_tiles[r]
+            nc.gpsimd.tensor_tensor(
+                out=q_round[:, :, 0:GPSIMD_TILES, :],
+                in0=q_round[:, :, 0:GPSIMD_TILES, :],
+                in1=gain[:, :, 0:GPSIMD_TILES].unsqueeze(3).to_broadcast(
+                    [P, HEADS, GPSIMD_TILES, HEAD_DIM]
+                ),
+                op=ALU.mult,
+            )
+            for i in range(GPSIMD_TILES, ROUND_TILES):
+                for h in range(HEADS):
+                    nc.scalar.activation(
+                        out=q_round[:, h, i, :],
+                        in_=q_round[:, h, i, :],
+                        func=ACT.Copy,
+                        scale=gain[:, h, i : i + 1],
+                    )
+
+        def store(r):
+            b = r // ROUNDS_PER_BATCH
+            n0 = (r % ROUNDS_PER_BATCH) * ROUND_TOKENS
+            nc.sync.dma_start(
+                out=out[b, :, n0 : n0 + ROUND_TOKENS, :].rearrange(
+                    "h (p i) d -> p h (i d)", i=ROUND_TILES
+                ),
+                in_=q_tiles[r][:].rearrange("p h i d -> p h (i d)"),
+            )
+
+        transpose(0)
+        for s in range(ROUNDS + 6):
+            if s + LOAD_AHEAD < ROUNDS:
+                load(s + LOAD_AHEAD)
+            if 0 <= s - 2 < ROUNDS:
+                project(s - 2)
+            if s + 1 < ROUNDS:
+                transpose(s + 1)
+            if 0 <= s - 6 < ROUNDS:
+                gains(s - 6)
+            if 0 <= s - 5 < ROUNDS:
+                sum_squares(s - 5)
+            if s < ROUNDS:
+                regroup(s)
+            if 0 <= s - 3 < ROUNDS:
+                add_bias(s - 3)
+            if 0 <= s - 4 < ROUNDS:
+                square(s - 4)
+            if 0 <= s - 5 < ROUNDS:
+                reciprocal_norm(s - 5)
+            if 0 <= s - 6 < ROUNDS:
+                scale(s - 6)
+            if 0 <= s - 1 < ROUNDS:
+                quantise(s - 1)
+            if 0 <= s - 6 < ROUNDS:
+                store(s - 6)

@@ -26,6 +26,9 @@ BANK_TILES = 2
 BANKS = ROUND_TILES // BANK_TILES
 LOAD_AHEAD = 6
 GPSIMD_TILES = 3
+SCALAR_SUM_TILES = 2
+VECTOR_SUM_TILES = ROUND_TILES - SCALAR_SUM_TILES
+STATS = 3
 
 FLOPS = 2 * BATCH * TOKENS * K * OUT_COLS
 
@@ -48,7 +51,8 @@ def tile_ufoattention_pb_t_kernel(tc, queries, Wq, bq, gamma, out):
         )
 
         x_tiles, xt_banks, grouped_tiles, code_tiles, scale_tiles = {}, {}, {}, {}, {}
-        acc_banks, q_tiles, square_tiles, sumsq_tiles, rnorm_tiles, gain_tiles = {}, {}, {}, {}, {}, {}
+        acc_banks, q_tiles, stats_tiles, sumsq_tiles, rnorm_tiles, gain_tiles = {}, {}, {}, {}, {}, {}
+        meansq_tiles = {}
 
         def load(r):
             x_tiles[r] = x_pool.tile([P, ROUND_TILES * K], BF16, name="x_sb")
@@ -159,14 +163,49 @@ def tile_ufoattention_pb_t_kernel(tc, queries, Wq, bq, gamma, out):
                     op=ALU.add,
                 )
 
-        def square(r):
-            square_tiles[r] = sq_pool.tile([P, HEADS, ROUND_TILES, HEAD_DIM], F32, name="squares")
-            nc.scalar.activation(out=square_tiles[r][:], in_=q_tiles[r][:], func=ACT.Square)
-
-        def sum_squares(r):
+        def scalar_sums(r):
             sumsq_tiles[r] = small.tile([P, HEADS, ROUND_TILES], F32, name="sumsq")
-            nc.vector.tensor_reduce(
-                out=sumsq_tiles[r][:], in_=square_tiles[r][:], axis=mybir.AxisListType.X, op=ALU.add
+            for i in range(SCALAR_SUM_TILES):
+                for h in range(HEADS):
+                    squares = sq_pool.tile([P, HEAD_DIM], F32, name="squares")
+                    nc.scalar.activation(
+                        out=squares[:],
+                        in_=q_tiles[r][:, h, i, :],
+                        func=ACT.Square,
+                        accum_out=sumsq_tiles[r][:, h, i : i + 1],
+                    )
+
+        def vector_stats(r):
+            stats_tiles[r] = small.tile([P, VECTOR_SUM_TILES, HEADS // 2, 2 * STATS], F32, name="stats")
+            for j in range(VECTOR_SUM_TILES):
+                for pair in range(HEADS // 2):
+                    nc.vector.bn_stats(
+                        out=stats_tiles[r][:, j, pair, :],
+                        in_=q_tiles[r][:, 2 * pair : 2 * pair + 2, SCALAR_SUM_TILES + j, :].rearrange(
+                            "p h d -> p d h"
+                        ),
+                    )
+
+        def stats_view(r, field):
+            return stats_tiles[r][:].rearrange("p j a (e c) -> p j (a e) c", e=2)[:, :, :, field]
+
+        def mean_squares(r):
+            meansq_tiles[r] = small.tile([P, VECTOR_SUM_TILES, HEADS], F32, name="meansq")
+            nc.vector.scalar_tensor_tensor(
+                out=meansq_tiles[r][:],
+                in0=stats_view(r, 1),
+                scalar=float(HEAD_DIM),
+                in1=stats_view(r, 1),
+                op0=ALU.mult,
+                op1=ALU.mult,
+            )
+
+        def vector_sums(r):
+            nc.vector.tensor_tensor(
+                out=sumsq_tiles[r][:, :, SCALAR_SUM_TILES:].rearrange("p h j -> p j h"),
+                in0=meansq_tiles[r][:],
+                in1=stats_view(r, 2),
+                op=ALU.add,
             )
 
         def reciprocal_norm(r):
@@ -218,16 +257,20 @@ def tile_ufoattention_pb_t_kernel(tc, queries, Wq, bq, gamma, out):
                 project(s - 2)
             if s + 1 < ROUNDS:
                 transpose(s + 1)
+            if 0 <= s - 5 < ROUNDS:
+                mean_squares(s - 5)
             if 0 <= s - 6 < ROUNDS:
                 gains(s - 6)
             if 0 <= s - 5 < ROUNDS:
-                sum_squares(s - 5)
+                vector_sums(s - 5)
+            if 0 <= s - 4 < ROUNDS:
+                vector_stats(s - 4)
             if s < ROUNDS:
                 regroup(s)
             if 0 <= s - 3 < ROUNDS:
                 add_bias(s - 3)
             if 0 <= s - 4 < ROUNDS:
-                square(s - 4)
+                scalar_sums(s - 4)
             if 0 <= s - 5 < ROUNDS:
                 reciprocal_norm(s - 5)
             if 0 <= s - 6 < ROUNDS:

@@ -1,3 +1,4 @@
+import math
 from contextlib import ExitStack
 
 import concourse.mybir as mybir
@@ -17,18 +18,14 @@ HEADS, HEAD_DIM = 4, 64
 OUT_COLS = HEADS * HEAD_DIM
 PACK = 4
 WORDS = K // 2
-
-ROUND_TILES = 4
-ROUND_TOKENS = P * ROUND_TILES
-ROUNDS_PER_BATCH = TOKENS // ROUND_TOKENS
-ROUNDS = BATCH * ROUNDS_PER_BATCH
 BANK_TILES = 2
-BANKS = ROUND_TILES // BANK_TILES
-LOAD_AHEAD = 6
-GPSIMD_TILES = 3
-SCALAR_SUM_TILES = 2
-VECTOR_SUM_TILES = ROUND_TILES - SCALAR_SUM_TILES
 STATS = 3
+
+UNITS = [2, 2, 4] + [8] * 14 + [4, 2, 2]
+LOAD_AHEAD = 6
+SCALAR_SUMS = {2: 1, 4: 2, 8: 4}
+GPSIMD_SCALES = {2: 1, 4: 3, 8: 6}
+VECTOR_SCALED = 3
 
 FLOPS = 2 * BATCH * TOKENS * K * OUT_COLS
 
@@ -38,37 +35,180 @@ def tile_ufoattention_pb_t_kernel(tc, queries, Wq, bq, gamma, out):
     with ExitStack() as ctx:
         ctx.enter_context(tc.manual_schedule())
         const = ctx.enter_context(tc.tile_pool(name="const", bufs=1))
-        x_pool = ctx.enter_context(tc.tile_pool(name="x", bufs=LOAD_AHEAD + 2))
-        mx_pool = ctx.enter_context(tc.tile_pool(name="mx", bufs=3))
-        q_pool = ctx.enter_context(tc.tile_pool(name="q", bufs=8))
-        small = ctx.enter_context(tc.tile_pool(name="small", bufs=10))
-        sq_pool = ctx.enter_context(tc.tile_pool(name="sq", bufs=3))
-        psum_t = ctx.enter_context(tc.psum_pool(name="psum_t", bufs=2 * BANKS))
-        psum_q = ctx.enter_context(tc.psum_pool(name="psum_q", bufs=2 * BANKS))
+        x_pool = ctx.enter_context(tc.tile_pool(name="x", bufs=LOAD_AHEAD + 3))
+        mx_pool = ctx.enter_context(tc.tile_pool(name="mx", bufs=2))
+        q_pool = ctx.enter_context(tc.tile_pool(name="q", bufs=5))
+        small = ctx.enter_context(tc.tile_pool(name="small", bufs=4))
+        sq_pool = ctx.enter_context(tc.tile_pool(name="sq", bufs=2))
+        psum_t = ctx.enter_context(tc.psum_pool(name="psum_t", bufs=4))
+        psum_q = ctx.enter_context(tc.psum_pool(name="psum_q", bufs=4))
 
-        x_rounds = queries.flatten_outer_dims().rearrange(
-            "(r p i) k -> r p (i k)", p=P, i=ROUND_TILES
-        )
+        x_rows = queries.flatten_outer_dims()
+        first_token = [P * sum(UNITS[:r]) for r in range(len(UNITS))]
+        rounds = len(UNITS)
 
         x_tiles, xt_banks, grouped_tiles, code_tiles, scale_tiles = {}, {}, {}, {}, {}
         acc_banks, q_tiles, stats_tiles, sumsq_tiles, rnorm_tiles, gain_tiles = {}, {}, {}, {}, {}, {}
-        meansq_tiles = {}
 
         def load(r):
-            x_tiles[r] = x_pool.tile([P, ROUND_TILES * K], BF16, name="x_sb")
-            nc.sync.dma_start(out=x_tiles[r][:], in_=x_rounds[r])
+            n = UNITS[r]
+            x_tiles[r] = x_pool.tile([P, n * K], BF16, name="x_sb")
+            nc.sync.dma_start(
+                out=x_tiles[r][:],
+                in_=x_rows[first_token[r] : first_token[r] + n * P, :].rearrange(
+                    "(p i) k -> p (i k)", i=n
+                ),
+            )
 
-        for r in range(LOAD_AHEAD):
-            load(r)
+        def transpose(r):
+            x_words = x_tiles[r][:].bitcast(F32)
+            xt_banks[r] = []
+            for bank in range(UNITS[r] // BANK_TILES):
+                xt = psum_t.tile([P, BANK_TILES, 2, P], F32, name="xt")
+                for i in range(BANK_TILES):
+                    first = (bank * BANK_TILES + i) * WORDS
+                    for u in range(2):
+                        nc.tensor.transpose(
+                            xt[:, i, u, :], x_words[:, first + u : first + WORDS : 2], ident[:]
+                        )
+                xt_banks[r].append(xt)
 
+        def regroup(r):
+            n = UNITS[r]
+            grouped_tiles[r] = mx_pool.tile([P, n * K], BF16, align_bytes=64, name="grouped")
+            grouped_words = grouped_tiles[r][:].bitcast(F32)
+            for bank, xt in enumerate(xt_banks[r]):
+                dst = grouped_words[
+                    :, bank * BANK_TILES * WORDS : (bank + 1) * BANK_TILES * WORDS
+                ].rearrange("p (i r u) -> p i r u", i=BANK_TILES, u=2)
+                nc.scalar.copy(out=dst, in_=xt[:].rearrange("p i u r -> p i r u"))
+
+        def quantise(r):
+            n = UNITS[r]
+            code_tiles[r] = mx_pool.tile([P, n * P], U32, align_bytes=64, name="codes")
+            scale_tiles[r] = mx_pool.tile([P, n * P], U8, align_bytes=64, name="scales")
+            nc.vector.quantize_mx(
+                out=code_tiles[r][:].bitcast(FP8X4),
+                scales=scale_tiles[r][:],
+                in_=grouped_tiles[r][:],
+            )
+
+        def project(r):
+            codes, scales = code_tiles[r], scale_tiles[r]
+            acc_banks[r] = []
+            for bank in range(UNITS[r] // BANK_TILES):
+                acc = psum_q.tile([P, BANK_TILES, OUT_COLS], F32, name="acc")
+                for i in range(BANK_TILES):
+                    cols = slice((bank * BANK_TILES + i) * P, (bank * BANK_TILES + i + 1) * P)
+                    nc.tensor.matmul_mx(
+                        out=acc[:, i, :],
+                        lhsT=codes[:, cols].bitcast(FP8X4),
+                        lhsT_scale=scales[:, cols],
+                        rhs=w_codes[:].bitcast(FP8X4),
+                        rhs_scale=w_scales[:],
+                        start=True,
+                        stop=True,
+                    )
+                acc_banks[r].append(acc)
+
+        def add_bias(r):
+            n = UNITS[r]
+            q_tiles[r] = q_pool.tile([P, HEADS, n, HEAD_DIM], F32, name="q_sb")
+            for bank, acc in enumerate(acc_banks[r]):
+                nc.vector.tensor_tensor(
+                    out=q_tiles[r][:, :, bank * BANK_TILES : (bank + 1) * BANK_TILES, :],
+                    in0=acc[:].rearrange("p i (h d) -> p h i d", h=HEADS),
+                    in1=bias_bank[:],
+                    op=ALU.add,
+                )
+
+        def scalar_sums(r):
+            sumsq_tiles[r] = small.tile([P, UNITS[r], HEADS], F32, name="sumsq")
+            for i in range(SCALAR_SUMS[UNITS[r]]):
+                for h in range(HEADS):
+                    squares = sq_pool.tile([P, HEAD_DIM], F32, name="squares")
+                    nc.scalar.activation(
+                        out=squares[:],
+                        in_=q_tiles[r][:, h, i, :],
+                        func=ACT.Square,
+                        accum_out=sumsq_tiles[r][:, i, h : h + 1],
+                    )
+
+        def vector_stats(r):
+            n, first = UNITS[r], SCALAR_SUMS[UNITS[r]]
+            stats_tiles[r] = small.tile([P, n - first, HEADS // 2, 2 * STATS], F32, name="stats")
+            for i in range(first, n):
+                for pair in range(HEADS // 2):
+                    nc.vector.bn_stats(
+                        out=stats_tiles[r][:, i - first, pair, :],
+                        in_=q_tiles[r][:, 2 * pair : 2 * pair + 2, i, :].rearrange("p h d -> p d h"),
+                    )
+
+        def mean_squares(r):
+            stats = stats_tiles[r][:].rearrange("p j a (e c) -> p (j a e) c", c=STATS)
+            nc.scalar.activation(
+                out=stats[:, :, 0], in_=stats[:, :, 1], func=ACT.Square, scale=math.sqrt(HEAD_DIM)
+            )
+
+        def vector_sums(r):
+            stats = stats_tiles[r][:].rearrange("p j a (e c) -> p (j a e) c", c=STATS)
+            nc.vector.tensor_reduce(
+                out=sumsq_tiles[r][:, SCALAR_SUMS[UNITS[r]] :, :].rearrange("p j h -> p (j h)"),
+                in_=stats[:, :, 0:STATS:2],
+                axis=mybir.AxisListType.X,
+                op=ALU.add,
+            )
+
+        def reciprocal_norm(r):
+            rnorm_tiles[r] = small.tile([P, UNITS[r], HEADS], F32, name="rnorm")
+            nc.scalar.activation(
+                out=rnorm_tiles[r][:], in_=sumsq_tiles[r][:], func=ACT.Abs_reciprocal_sqrt
+            )
+
+        def gains(r):
+            n = UNITS[r]
+            gain_tiles[r] = small.tile([P, n, HEADS], F32, name="gain")
+            nc.vector.tensor_tensor(
+                out=gain_tiles[r][:],
+                in0=rnorm_tiles[r][:],
+                in1=gamma_sb[:].unsqueeze(1).to_broadcast([P, n, HEADS]),
+                op=ALU.mult,
+            )
+
+        def scale_tiles_of(engine, r, first, last):
+            gain = gain_tiles[r][:, first:last, :].rearrange("p i h -> p h i")
+            engine.tensor_tensor(
+                out=q_tiles[r][:, :, first:last, :],
+                in0=q_tiles[r][:, :, first:last, :],
+                in1=gain.unsqueeze(3).to_broadcast([P, HEADS, last - first, HEAD_DIM]),
+                op=ALU.mult,
+            )
+
+        def scalar_scale(r, first, last):
+            for i in range(first, last):
+                for h in range(HEADS):
+                    nc.scalar.activation(
+                        out=q_tiles[r][:, h, i, :],
+                        in_=q_tiles[r][:, h, i, :],
+                        func=ACT.Copy,
+                        scale=gain_tiles[r][:, i, h : h + 1],
+                    )
+
+        def store(r):
+            n = UNITS[r]
+            b, n0 = first_token[r] // TOKENS, first_token[r] % TOKENS
+            nc.sync.dma_start(
+                out=out[b, :, n0 : n0 + n * P, :].rearrange("h (p i) d -> p h (i d)", i=n),
+                in_=q_tiles[r][:].rearrange("p h i d -> p h (i d)"),
+            )
+
+        load(0)
+        load(1)
         ident = const.tile([P, P], F32)
         make_identity(nc, ident[:])
 
         w_raw = const.tile([P, PACK, OUT_COLS], BF16)
-        nc.scalar.dma_start(
-            out=w_raw[:],
-            in_=Wq.rearrange("(p t) c -> p t c", t=PACK),
-        )
+        nc.scalar.dma_start(out=w_raw[:], in_=Wq.rearrange("(p t) c -> p t c", t=PACK))
         bias_bf = const.tile([P, OUT_COLS], BF16)
         nc.scalar.dma_start(out=bias_bf[:], in_=bq.partition_broadcast(P))
         gamma_bf = const.tile([P, HEADS], BF16)
@@ -76,6 +216,8 @@ def tile_ufoattention_pb_t_kernel(tc, queries, Wq, bq, gamma, out):
             out=gamma_bf[:],
             in_=gamma.rearrange("a h b c -> (a h b c)").partition_broadcast(P),
         )
+        for r in range(2, LOAD_AHEAD + 2):
+            load(r)
 
         one = const.tile([P, 1], F32)
         nc.vector.memset(one[:], 1.0)
@@ -96,186 +238,40 @@ def tile_ufoattention_pb_t_kernel(tc, queries, Wq, bq, gamma, out):
                 out=bias_bank[:, :, i, :],
                 in_=bias_bf[:].rearrange("p (h d) -> p h d", h=HEADS),
             )
-        gamma_round = const.tile([P, HEADS, ROUND_TILES], F32)
-        nc.vector.tensor_copy(
-            out=gamma_round[:],
-            in_=gamma_bf[:].unsqueeze(2).to_broadcast([P, HEADS, ROUND_TILES]),
-        )
-
-        def transpose(r):
-            x_words = x_tiles[r][:].bitcast(F32)
-            xt_banks[r] = []
-            for bank in range(BANKS):
-                xt = psum_t.tile([P, BANK_TILES, 2, P], F32, name="xt")
-                for i in range(BANK_TILES):
-                    for u in range(2):
-                        first = (bank * BANK_TILES + i) * WORDS
-                        nc.tensor.transpose(
-                            xt[:, i, u, :], x_words[:, first + u : first + WORDS : 2], ident[:]
-                        )
-                xt_banks[r].append(xt)
-
-        def regroup(r):
-            grouped_tiles[r] = mx_pool.tile([P, ROUND_TILES * K], BF16, align_bytes=64, name="grouped")
-            grouped_words = grouped_tiles[r][:].bitcast(F32)
-            for bank, xt in enumerate(xt_banks[r]):
-                dst = grouped_words[
-                    :, bank * BANK_TILES * WORDS : (bank + 1) * BANK_TILES * WORDS
-                ].rearrange("p (i r u) -> p i r u", i=BANK_TILES, u=2)
-                src = xt[:].rearrange("p i u r -> p i r u")
-                nc.scalar.copy(out=dst, in_=src)
-
-        def quantise(r):
-            code_tiles[r] = mx_pool.tile([P, ROUND_TILES * P], U32, align_bytes=64, name="codes")
-            scale_tiles[r] = mx_pool.tile([P, ROUND_TILES * P], U8, align_bytes=64, name="scales")
-            nc.vector.quantize_mx(
-                out=code_tiles[r][:].bitcast(FP8X4),
-                scales=scale_tiles[r][:],
-                in_=grouped_tiles[r][:],
-            )
-
-        def project(r):
-            codes, scales = code_tiles[r], scale_tiles[r]
-            acc_banks[r] = []
-            for bank in range(BANKS):
-                acc = psum_q.tile([P, BANK_TILES, OUT_COLS], F32, name="acc")
-                for i in range(BANK_TILES):
-                    cols = slice((bank * BANK_TILES + i) * P, (bank * BANK_TILES + i + 1) * P)
-                    nc.tensor.matmul_mx(
-                        out=acc[:, i, :],
-                        lhsT=codes[:, cols].bitcast(FP8X4),
-                        lhsT_scale=scales[:, cols],
-                        rhs=w_codes[:].bitcast(FP8X4),
-                        rhs_scale=w_scales[:],
-                        start=True,
-                        stop=True,
-                    )
-                acc_banks[r].append(acc)
-
-        def add_bias(r):
-            q_tiles[r] = q_pool.tile([P, HEADS, ROUND_TILES, HEAD_DIM], F32, name="q_sb")
-            q_round = q_tiles[r]
-            for bank, acc in enumerate(acc_banks[r]):
-                nc.vector.tensor_tensor(
-                    out=q_round[:, :, bank * BANK_TILES : (bank + 1) * BANK_TILES, :],
-                    in0=acc[:].rearrange("p i (h d) -> p h i d", h=HEADS),
-                    in1=bias_bank[:],
-                    op=ALU.add,
-                )
-
-        def scalar_sums(r):
-            sumsq_tiles[r] = small.tile([P, HEADS, ROUND_TILES], F32, name="sumsq")
-            for i in range(SCALAR_SUM_TILES):
-                for h in range(HEADS):
-                    squares = sq_pool.tile([P, HEAD_DIM], F32, name="squares")
-                    nc.scalar.activation(
-                        out=squares[:],
-                        in_=q_tiles[r][:, h, i, :],
-                        func=ACT.Square,
-                        accum_out=sumsq_tiles[r][:, h, i : i + 1],
-                    )
-
-        def vector_stats(r):
-            stats_tiles[r] = small.tile([P, VECTOR_SUM_TILES, HEADS // 2, 2 * STATS], F32, name="stats")
-            for j in range(VECTOR_SUM_TILES):
-                for pair in range(HEADS // 2):
-                    nc.vector.bn_stats(
-                        out=stats_tiles[r][:, j, pair, :],
-                        in_=q_tiles[r][:, 2 * pair : 2 * pair + 2, SCALAR_SUM_TILES + j, :].rearrange(
-                            "p h d -> p d h"
-                        ),
-                    )
-
-        def stats_view(r, field):
-            return stats_tiles[r][:].rearrange("p j a (e c) -> p j (a e) c", e=2)[:, :, :, field]
-
-        def mean_squares(r):
-            meansq_tiles[r] = small.tile([P, VECTOR_SUM_TILES, HEADS], F32, name="meansq")
-            nc.vector.scalar_tensor_tensor(
-                out=meansq_tiles[r][:],
-                in0=stats_view(r, 1),
-                scalar=float(HEAD_DIM),
-                in1=stats_view(r, 1),
-                op0=ALU.mult,
-                op1=ALU.mult,
-            )
-
-        def vector_sums(r):
-            nc.vector.tensor_tensor(
-                out=sumsq_tiles[r][:, :, SCALAR_SUM_TILES:].rearrange("p h j -> p j h"),
-                in0=meansq_tiles[r][:],
-                in1=stats_view(r, 2),
-                op=ALU.add,
-            )
-
-        def reciprocal_norm(r):
-            rnorm_tiles[r] = small.tile([P, HEADS, ROUND_TILES], F32, name="rnorm")
-            nc.scalar.activation(
-                out=rnorm_tiles[r][:], in_=sumsq_tiles[r][:], func=ACT.Abs_reciprocal_sqrt
-            )
-
-        def gains(r):
-            gain_tiles[r] = small.tile([P, HEADS, ROUND_TILES], F32, name="gain")
-            nc.vector.tensor_tensor(
-                out=gain_tiles[r][:], in0=rnorm_tiles[r][:], in1=gamma_round[:], op=ALU.mult
-            )
-
-        def scale(r):
-            q_round, gain = q_tiles[r], gain_tiles[r]
-            nc.gpsimd.tensor_tensor(
-                out=q_round[:, :, 0:GPSIMD_TILES, :],
-                in0=q_round[:, :, 0:GPSIMD_TILES, :],
-                in1=gain[:, :, 0:GPSIMD_TILES].unsqueeze(3).to_broadcast(
-                    [P, HEADS, GPSIMD_TILES, HEAD_DIM]
-                ),
-                op=ALU.mult,
-            )
-            for i in range(GPSIMD_TILES, ROUND_TILES):
-                for h in range(HEADS):
-                    nc.scalar.activation(
-                        out=q_round[:, h, i, :],
-                        in_=q_round[:, h, i, :],
-                        func=ACT.Copy,
-                        scale=gain[:, h, i : i + 1],
-                    )
-
-        def store(r):
-            b = r // ROUNDS_PER_BATCH
-            n0 = (r % ROUNDS_PER_BATCH) * ROUND_TOKENS
-            nc.sync.dma_start(
-                out=out[b, :, n0 : n0 + ROUND_TOKENS, :].rearrange(
-                    "h (p i) d -> p h (i d)", i=ROUND_TILES
-                ),
-                in_=q_tiles[r][:].rearrange("p h i d -> p h (i d)"),
-            )
+        gamma_sb = const.tile([P, HEADS], F32)
+        nc.vector.tensor_copy(out=gamma_sb[:], in_=gamma_bf[:])
 
         transpose(0)
-        for s in range(ROUNDS + 6):
-            if s + LOAD_AHEAD < ROUNDS:
-                load(s + LOAD_AHEAD)
-            if 0 <= s - 2 < ROUNDS:
-                project(s - 2)
-            if s + 1 < ROUNDS:
-                transpose(s + 1)
-            if 0 <= s - 5 < ROUNDS:
-                mean_squares(s - 5)
-            if 0 <= s - 6 < ROUNDS:
-                gains(s - 6)
-            if 0 <= s - 5 < ROUNDS:
-                vector_sums(s - 5)
-            if 0 <= s - 4 < ROUNDS:
-                vector_stats(s - 4)
-            if s < ROUNDS:
-                regroup(s)
-            if 0 <= s - 3 < ROUNDS:
-                add_bias(s - 3)
-            if 0 <= s - 4 < ROUNDS:
-                scalar_sums(s - 4)
-            if 0 <= s - 5 < ROUNDS:
-                reciprocal_norm(s - 5)
-            if 0 <= s - 6 < ROUNDS:
-                scale(s - 6)
-            if 0 <= s - 1 < ROUNDS:
-                quantise(s - 1)
-            if 0 <= s - 6 < ROUNDS:
-                store(s - 6)
+        transpose(1)
+        regroup(0)
+        for s in range(rounds + 2):
+            if s + 2 + LOAD_AHEAD < rounds:
+                load(s + 2 + LOAD_AHEAD)
+            if s < rounds:
+                quantise(s)
+                project(s)
+            if s + 1 < rounds:
+                regroup(s + 1)
+            if s + 2 < rounds:
+                transpose(s + 2)
+            if 0 <= s - 2:
+                gains(s - 2)
+                if s - 2 < rounds - VECTOR_SCALED:
+                    first = GPSIMD_SCALES[UNITS[s - 2]]
+                    scale_tiles_of(nc.gpsimd, s - 2, 0, first)
+                else:
+                    first = UNITS[s - 2] // 2
+                    scale_tiles_of(nc.vector, s - 2, 0, first)
+            if 0 <= s - 1 < rounds:
+                vector_stats(s - 1)
+                scalar_sums(s - 1)
+            if s < rounds:
+                add_bias(s)
+            if 0 <= s - 1 < rounds:
+                mean_squares(s - 1)
+                vector_sums(s - 1)
+            if 0 <= s - 2:
+                scalar_scale(s - 2, first, UNITS[s - 2])
+                store(s - 2)
+            if 0 <= s - 1 < rounds:
+                reciprocal_norm(s - 1)

@@ -39,7 +39,7 @@ def tile_ufoattention_pb_t_kernel(tc, queries, Wq, bq, gamma, out):
         mx_pool = ctx.enter_context(tc.tile_pool(name="mx", bufs=2))
         q_pool = ctx.enter_context(tc.tile_pool(name="q", bufs=5))
         small = ctx.enter_context(tc.tile_pool(name="small", bufs=4))
-        sq_pool = ctx.enter_context(tc.tile_pool(name="sq", bufs=2))
+        sq_pool = ctx.enter_context(tc.tile_pool(name="sq", bufs=3))
         psum_t = ctx.enter_context(tc.psum_pool(name="psum_t", bufs=4))
         psum_q = ctx.enter_context(tc.psum_pool(name="psum_q", bufs=4))
 
@@ -124,11 +124,12 @@ def tile_ufoattention_pb_t_kernel(tc, queries, Wq, bq, gamma, out):
 
         def scalar_sums(r):
             sumsq_tiles[r] = small.tile([P, UNITS[r], HEADS], F32, name="sumsq")
-            for i in range(SCALAR_SUMS[UNITS[r]]):
+            count = SCALAR_SUMS[UNITS[r]]
+            squares = sq_pool.tile([P, HEADS, count, HEAD_DIM], F32, name="squares")
+            for i in range(count):
                 for h in range(HEADS):
-                    squares = sq_pool.tile([P, HEAD_DIM], F32, name="squares")
                     nc.scalar.activation(
-                        out=squares[:],
+                        out=squares[:, h, i, :],
                         in_=q_tiles[r][:, h, i, :],
                         func=ACT.Square,
                         accum_out=sumsq_tiles[r][:, i, h : h + 1],

@@ -21,11 +21,11 @@ WORDS = K // 2
 BANK_TILES = 2
 STATS = 3
 
-UNITS = [2, 2, 4] + [8] * 14 + [4, 2, 2]
+UNITS = [4, 4] + [8] * 14 + [4, 2, 2]
 LOAD_AHEAD = 6
 SCALAR_SUMS = {2: 1, 4: 2, 8: 4}
 GPSIMD_SCALES = {2: 1, 4: 3, 8: 6}
-VECTOR_SCALED = 3
+VECTOR_SCALED = 4
 
 FLOPS = 2 * BATCH * TOKENS * K * OUT_COLS
 
@@ -49,21 +49,24 @@ def tile_ufoattention_pb_t_kernel(tc, queries, Wq, bq, gamma, out):
 
         x_tiles, xt_banks, grouped_tiles, code_tiles, scale_tiles = {}, {}, {}, {}, {}
         acc_banks, q_tiles, stats_tiles, sumsq_tiles, rnorm_tiles, gain_tiles = {}, {}, {}, {}, {}, {}
+        square_tiles = {}
 
-        def load(r):
+        def load(r, pieces=1):
             n = UNITS[r]
             x_tiles[r] = x_pool.tile([P, n * K], BF16, name="x_sb")
-            nc.sync.dma_start(
-                out=x_tiles[r][:],
-                in_=x_rows[first_token[r] : first_token[r] + n * P, :].rearrange(
-                    "(p i) k -> p (i k)", i=n
-                ),
-            )
+            rows = x_rows[first_token[r] : first_token[r] + n * P, :].rearrange("(p i) k -> p (i k)", i=n)
+            width = n * K // pieces
+            for j in range(pieces):
+                nc.sync.dma_start(
+                    out=x_tiles[r][:, j * width : (j + 1) * width],
+                    in_=rows[:, j * width : (j + 1) * width],
+                )
 
-        def transpose(r):
+        def transpose(r, banks):
+            if not banks:
+                return
             x_words = x_tiles[r][:].bitcast(F32)
-            xt_banks[r] = []
-            for bank in range(UNITS[r] // BANK_TILES):
+            for bank in banks:
                 xt = psum_t.tile([P, BANK_TILES, 2, P], F32, name="xt")
                 for i in range(BANK_TILES):
                     first = (bank * BANK_TILES + i) * WORDS
@@ -71,32 +74,38 @@ def tile_ufoattention_pb_t_kernel(tc, queries, Wq, bq, gamma, out):
                         nc.tensor.transpose(
                             xt[:, i, u, :], x_words[:, first + u : first + WORDS : 2], ident[:]
                         )
-                xt_banks[r].append(xt)
+                xt_banks.setdefault(r, []).append(xt)
 
-        def regroup(r):
+        def regroup(r, part, parts_n):
             n = UNITS[r]
-            grouped_tiles[r] = mx_pool.tile([P, n * K], BF16, align_bytes=64, name="grouped")
+            if r not in grouped_tiles:
+                grouped_tiles[r] = mx_pool.tile([P, n * K], BF16, align_bytes=64, name="grouped")
             grouped_words = grouped_tiles[r][:].bitcast(F32)
-            for bank, xt in enumerate(xt_banks[r]):
+            count = n // BANK_TILES
+            for bank in range(count * part // parts_n, count * (part + 1) // parts_n):
+                xt = xt_banks[r][bank]
                 dst = grouped_words[
                     :, bank * BANK_TILES * WORDS : (bank + 1) * BANK_TILES * WORDS
                 ].rearrange("p (i r u) -> p i r u", i=BANK_TILES, u=2)
                 nc.scalar.copy(out=dst, in_=xt[:].rearrange("p i u r -> p i r u"))
 
-        def quantise(r):
+        def quantise(r, first=0, last=None):
             n = UNITS[r]
-            code_tiles[r] = mx_pool.tile([P, n * P], U32, align_bytes=64, name="codes")
-            scale_tiles[r] = mx_pool.tile([P, n * P], U8, align_bytes=64, name="scales")
+            last = n if last is None else last
+            if r not in code_tiles:
+                code_tiles[r] = mx_pool.tile([P, n * P], U32, align_bytes=64, name="codes")
+                scale_tiles[r] = mx_pool.tile([P, n * P], U8, align_bytes=64, name="scales")
             nc.vector.quantize_mx(
-                out=code_tiles[r][:].bitcast(FP8X4),
-                scales=scale_tiles[r][:],
-                in_=grouped_tiles[r][:],
+                out=code_tiles[r][:, first * P : last * P].bitcast(FP8X4),
+                scales=scale_tiles[r][:, first * P : last * P],
+                in_=grouped_tiles[r][:, first * K : last * K],
             )
 
-        def project(r):
+        def project(r, banks):
+            if not banks:
+                return
             codes, scales = code_tiles[r], scale_tiles[r]
-            acc_banks[r] = []
-            for bank in range(UNITS[r] // BANK_TILES):
+            for bank in banks:
                 acc = psum_q.tile([P, BANK_TILES, OUT_COLS], F32, name="acc")
                 for i in range(BANK_TILES):
                     cols = slice((bank * BANK_TILES + i) * P, (bank * BANK_TILES + i + 1) * P)
@@ -109,12 +118,14 @@ def tile_ufoattention_pb_t_kernel(tc, queries, Wq, bq, gamma, out):
                         start=True,
                         stop=True,
                     )
-                acc_banks[r].append(acc)
+                acc_banks.setdefault(r, []).append(acc)
 
-        def add_bias(r):
+        def add_bias(r, banks):
             n = UNITS[r]
-            q_tiles[r] = q_pool.tile([P, HEADS, n, HEAD_DIM], F32, name="q_sb")
-            for bank, acc in enumerate(acc_banks[r]):
+            if r not in q_tiles:
+                q_tiles[r] = q_pool.tile([P, HEADS, n, HEAD_DIM], F32, name="q_sb")
+            for bank in banks:
+                acc = acc_banks[r][bank]
                 nc.vector.tensor_tensor(
                     out=q_tiles[r][:, :, bank * BANK_TILES : (bank + 1) * BANK_TILES, :],
                     in0=acc[:].rearrange("p i (h d) -> p h i d", h=HEADS),
@@ -122,23 +133,26 @@ def tile_ufoattention_pb_t_kernel(tc, queries, Wq, bq, gamma, out):
                     op=ALU.add,
                 )
 
-        def scalar_sums(r):
-            sumsq_tiles[r] = small.tile([P, UNITS[r], HEADS], F32, name="sumsq")
-            count = SCALAR_SUMS[UNITS[r]]
-            squares = sq_pool.tile([P, HEADS, count, HEAD_DIM], F32, name="squares")
-            for i in range(count):
+        def scalar_sums(r, first, last):
+            if r not in sumsq_tiles:
+                n = UNITS[r]
+                sumsq_tiles[r] = small.tile([P, n, HEADS], F32, name="sumsq")
+                square_tiles[r] = sq_pool.tile([P, HEADS, SCALAR_SUMS[n], HEAD_DIM], F32, name="squares")
+            for i in range(first, last):
                 for h in range(HEADS):
                     nc.scalar.activation(
-                        out=squares[:, h, i, :],
+                        out=square_tiles[r][:, h, i, :],
                         in_=q_tiles[r][:, h, i, :],
                         func=ACT.Square,
                         accum_out=sumsq_tiles[r][:, i, h : h + 1],
                     )
 
-        def vector_stats(r):
+        def vector_stats(r, part, parts_n):
             n, first = UNITS[r], SCALAR_SUMS[UNITS[r]]
-            stats_tiles[r] = small.tile([P, n - first, HEADS // 2, 2 * STATS], F32, name="stats")
-            for i in range(first, n):
+            if r not in stats_tiles:
+                stats_tiles[r] = small.tile([P, n - first, HEADS // 2, 2 * STATS], F32, name="stats")
+            count = n - first
+            for i in range(first + count * part // parts_n, first + count * (part + 1) // parts_n):
                 for pair in range(HEADS // 2):
                     nc.vector.bn_stats(
                         out=stats_tiles[r][:, i - first, pair, :],
@@ -234,45 +248,64 @@ def tile_ufoattention_pb_t_kernel(tc, queries, Wq, bq, gamma, out):
             in_=w_grouped[:].rearrange("p c t -> p (c t)"),
         )
         bias_bank = const.tile([P, HEADS, BANK_TILES, HEAD_DIM], F32)
-        for i in range(BANK_TILES):
-            nc.vector.tensor_copy(
-                out=bias_bank[:, :, i, :],
-                in_=bias_bf[:].rearrange("p (h d) -> p h d", h=HEADS),
-            )
         gamma_sb = const.tile([P, HEADS], F32)
-        nc.vector.tensor_copy(out=gamma_sb[:], in_=gamma_bf[:])
 
-        transpose(0)
-        transpose(1)
-        regroup(0)
+        def bias_and_gains():
+            for i in range(BANK_TILES):
+                nc.vector.tensor_copy(
+                    out=bias_bank[:, :, i, :],
+                    in_=bias_bf[:].rearrange("p (h d) -> p h d", h=HEADS),
+                )
+            nc.vector.tensor_copy(out=gamma_sb[:], in_=gamma_bf[:])
+
+        def have(r, banks):
+            return [b for b in banks if 0 <= r < rounds and b < UNITS[r] // BANK_TILES]
+
+        def live(r):
+            return 0 <= r < rounds
+
+        transpose(0, have(0, [0, 1, 2, 3]))
+        transpose(1, have(1, [0, 1, 2, 3]))
+        regroup(0, 0, 1)
         for s in range(rounds + 2):
-            if s + 2 + LOAD_AHEAD < rounds:
+            if live(s + 2 + LOAD_AHEAD):
                 load(s + 2 + LOAD_AHEAD)
-            if s < rounds:
-                quantise(s)
-                project(s)
-            if s + 1 < rounds:
-                regroup(s + 1)
-            if s + 2 < rounds:
-                transpose(s + 2)
-            if 0 <= s - 2:
+            if live(s - 2):
                 gains(s - 2)
-                if s - 2 < rounds - VECTOR_SCALED:
-                    first = GPSIMD_SCALES[UNITS[s - 2]]
-                    scale_tiles_of(nc.gpsimd, s - 2, 0, first)
-                else:
-                    first = UNITS[s - 2] // 2
-                    scale_tiles_of(nc.vector, s - 2, 0, first)
-            if 0 <= s - 1 < rounds:
-                vector_stats(s - 1)
-                scalar_sums(s - 1)
-            if s < rounds:
-                add_bias(s)
-            if 0 <= s - 1 < rounds:
+                vector_scaled = s - 2 >= rounds - VECTOR_SCALED
+                scaled = UNITS[s - 2] // 2 if vector_scaled else GPSIMD_SCALES[UNITS[s - 2]]
+                middle = (scaled + UNITS[s - 2] + 1) // 2
+            if live(s - 2) and not vector_scaled:
+                scale_tiles_of(nc.gpsimd, s - 2, 0, scaled)
+            if live(s):
+                quantise(s)
+            if live(s + 1):
+                regroup(s + 1, 0, 1)
+            if s == 0:
+                bias_and_gains()
+            if live(s - 1):
+                vector_stats(s - 1, 0, 1)
+            if live(s - 1):
+                scalar_sums(s - 1, SCALAR_SUMS[UNITS[s - 1]] * 0 // 2, SCALAR_SUMS[UNITS[s - 1]] * (0 + 1) // 2)
+            if live(s - 1):
                 mean_squares(s - 1)
+            if live(s - 1):
+                scalar_sums(s - 1, SCALAR_SUMS[UNITS[s - 1]] * 1 // 2, SCALAR_SUMS[UNITS[s - 1]] * (1 + 1) // 2)
+            project(s, have(s, [0, 1, 2, 3]))
+            transpose(s + 2, have(s + 2, [0, 1, 2, 3]))
+            if have(s, [0, 1]):
+                add_bias(s, have(s, [0, 1]))
+            if live(s - 1):
                 vector_sums(s - 1)
-            if 0 <= s - 2:
-                scalar_scale(s - 2, first, UNITS[s - 2])
-                store(s - 2)
-            if 0 <= s - 1 < rounds:
+            if have(s, [2, 3]):
+                add_bias(s, have(s, [2, 3]))
+            if live(s - 2) and vector_scaled:
+                scale_tiles_of(nc.vector, s - 2, 0, scaled)
+            if live(s - 2):
+                scalar_scale(s - 2, scaled, middle)
+            if live(s - 1):
                 reciprocal_norm(s - 1)
+            if live(s - 2):
+                scalar_scale(s - 2, middle, UNITS[s - 2])
+            if live(s - 2):
+                store(s - 2)

@@ -23,7 +23,7 @@ STATS = 3
 
 UNITS = [4, 4] + [8] * 14 + [4, 2, 2]
 LOAD_AHEAD = 6
-SCALAR_SUMS = {2: 1, 4: 2, 8: 4}
+SCALAR_PAIRS = {2: 2, 4: 4, 8: 7}
 GPSIMD_SCALES = {2: 1, 4: 3, 8: 6}
 VECTOR_SCALED = 4
 
@@ -35,7 +35,7 @@ def tile_ufoattention_pb_t_kernel(tc, queries, Wq, bq, gamma, out):
     with ExitStack() as ctx:
         ctx.enter_context(tc.manual_schedule())
         const = ctx.enter_context(tc.tile_pool(name="const", bufs=1))
-        x_pool = ctx.enter_context(tc.tile_pool(name="x", bufs=LOAD_AHEAD + 3))
+        x_pool = ctx.enter_context(tc.tile_pool(name="x", bufs=LOAD_AHEAD + 5))
         mx_pool = ctx.enter_context(tc.tile_pool(name="mx", bufs=2))
         q_pool = ctx.enter_context(tc.tile_pool(name="q", bufs=5))
         small = ctx.enter_context(tc.tile_pool(name="small", bufs=4))
@@ -133,49 +133,48 @@ def tile_ufoattention_pb_t_kernel(tc, queries, Wq, bq, gamma, out):
                     op=ALU.add,
                 )
 
-        def scalar_sums(r, first, last):
+        def scalar_sums(r, half):
+            n, pairs = UNITS[r], SCALAR_PAIRS[UNITS[r]]
             if r not in sumsq_tiles:
-                n = UNITS[r]
-                sumsq_tiles[r] = small.tile([P, n, HEADS], F32, name="sumsq")
-                square_tiles[r] = sq_pool.tile([P, HEADS, SCALAR_SUMS[n], HEAD_DIM], F32, name="squares")
-            for i in range(first, last):
-                for h in range(HEADS):
-                    nc.scalar.activation(
-                        out=square_tiles[r][:, h, i, :],
-                        in_=q_tiles[r][:, h, i, :],
-                        func=ACT.Square,
-                        accum_out=sumsq_tiles[r][:, i, h : h + 1],
-                    )
+                sumsq_tiles[r] = small.tile([P, n * HEADS], F32, name="sumsq")
+                square_tiles[r] = sq_pool.tile([P, 2 * pairs, HEAD_DIM], F32, name="squares")
+            for j in range(2 * pairs * half // 2, 2 * pairs * (half + 1) // 2):
+                nc.scalar.activation(
+                    out=square_tiles[r][:, j, :],
+                    in_=q_tiles[r][:, j % HEADS, j // HEADS, :],
+                    func=ACT.Square,
+                    accum_out=sumsq_tiles[r][:, j : j + 1],
+                )
 
         def vector_stats(r, part, parts_n):
-            n, first = UNITS[r], SCALAR_SUMS[UNITS[r]]
+            n, first = UNITS[r], SCALAR_PAIRS[UNITS[r]]
             if r not in stats_tiles:
-                stats_tiles[r] = small.tile([P, n - first, HEADS // 2, 2 * STATS], F32, name="stats")
-            count = n - first
-            for i in range(first + count * part // parts_n, first + count * (part + 1) // parts_n):
-                for pair in range(HEADS // 2):
-                    nc.vector.bn_stats(
-                        out=stats_tiles[r][:, i - first, pair, :],
-                        in_=q_tiles[r][:, 2 * pair : 2 * pair + 2, i, :].rearrange("p h d -> p d h"),
-                    )
+                stats_tiles[r] = small.tile([P, 2 * n - first, 2 * STATS], F32, name="stats")
+            count = 2 * n - first
+            for j in range(first + count * part // parts_n, first + count * (part + 1) // parts_n):
+                i, h = j // 2, 2 * (j % 2)
+                nc.vector.bn_stats(
+                    out=stats_tiles[r][:, j - first, :],
+                    in_=q_tiles[r][:, h : h + 2, i, :].rearrange("p h d -> p d h"),
+                )
 
         def mean_squares(r):
-            stats = stats_tiles[r][:].rearrange("p j a (e c) -> p (j a e) c", c=STATS)
+            stats = stats_tiles[r][:].rearrange("p j (e c) -> p (j e) c", c=STATS)
             nc.scalar.activation(
                 out=stats[:, :, 0], in_=stats[:, :, 1], func=ACT.Square, scale=math.sqrt(HEAD_DIM)
             )
 
         def vector_sums(r):
-            stats = stats_tiles[r][:].rearrange("p j a (e c) -> p (j a e) c", c=STATS)
+            stats = stats_tiles[r][:].rearrange("p j (e c) -> p (j e) c", c=STATS)
             nc.vector.tensor_reduce(
-                out=sumsq_tiles[r][:, SCALAR_SUMS[UNITS[r]] :, :].rearrange("p j h -> p (j h)"),
+                out=sumsq_tiles[r][:, 2 * SCALAR_PAIRS[UNITS[r]] :],
                 in_=stats[:, :, 0:STATS:2],
                 axis=mybir.AxisListType.X,
                 op=ALU.add,
             )
 
         def reciprocal_norm(r):
-            rnorm_tiles[r] = small.tile([P, UNITS[r], HEADS], F32, name="rnorm")
+            rnorm_tiles[r] = small.tile([P, UNITS[r] * HEADS], F32, name="rnorm")
             nc.scalar.activation(
                 out=rnorm_tiles[r][:], in_=sumsq_tiles[r][:], func=ACT.Abs_reciprocal_sqrt
             )
@@ -185,7 +184,7 @@ def tile_ufoattention_pb_t_kernel(tc, queries, Wq, bq, gamma, out):
             gain_tiles[r] = small.tile([P, n, HEADS], F32, name="gain")
             nc.vector.tensor_tensor(
                 out=gain_tiles[r][:],
-                in0=rnorm_tiles[r][:],
+                in0=rnorm_tiles[r][:].rearrange("p (i h) -> p i h", h=HEADS),
                 in1=gamma_sb[:].unsqueeze(1).to_broadcast([P, n, HEADS]),
                 op=ALU.mult,
             )
@@ -264,21 +263,29 @@ def tile_ufoattention_pb_t_kernel(tc, queries, Wq, bq, gamma, out):
         def live(r):
             return 0 <= r < rounds
 
+        warm = psum_t.tile([P, BANK_TILES, 2, P], F32, name="xt")
+        for i in range(5):
+            nc.tensor.matmul(warm[:, i % 2, 0, :], lhsT=ident[:], rhs=ident[:], start=True, stop=True)
         transpose(0, have(0, [0, 1, 2, 3]))
         transpose(1, have(1, [0, 1, 2, 3]))
         regroup(0, 0, 1)
         for s in range(rounds + 2):
             if live(s + 2 + LOAD_AHEAD):
                 load(s + 2 + LOAD_AHEAD)
-            if live(s - 2):
+            if live(s - 2) and s >= 4:
+                gains(s - 2)
+                vector_scaled = s - 2 >= rounds - VECTOR_SCALED
+                scaled = UNITS[s - 2] // 2 if vector_scaled else GPSIMD_SCALES[UNITS[s - 2]]
+                middle = (scaled + UNITS[s - 2] + 1) // 2
+            if live(s):
+                quantise(s)
+            if live(s - 2) and s < 4:
                 gains(s - 2)
                 vector_scaled = s - 2 >= rounds - VECTOR_SCALED
                 scaled = UNITS[s - 2] // 2 if vector_scaled else GPSIMD_SCALES[UNITS[s - 2]]
                 middle = (scaled + UNITS[s - 2] + 1) // 2
             if live(s - 2) and not vector_scaled:
                 scale_tiles_of(nc.gpsimd, s - 2, 0, scaled)
-            if live(s):
-                quantise(s)
             if live(s + 1):
                 regroup(s + 1, 0, 1)
             if s == 0:
@@ -286,11 +293,11 @@ def tile_ufoattention_pb_t_kernel(tc, queries, Wq, bq, gamma, out):
             if live(s - 1):
                 vector_stats(s - 1, 0, 1)
             if live(s - 1):
-                scalar_sums(s - 1, SCALAR_SUMS[UNITS[s - 1]] * 0 // 2, SCALAR_SUMS[UNITS[s - 1]] * (0 + 1) // 2)
+                scalar_sums(s - 1, 0)
             if live(s - 1):
                 mean_squares(s - 1)
             if live(s - 1):
-                scalar_sums(s - 1, SCALAR_SUMS[UNITS[s - 1]] * 1 // 2, SCALAR_SUMS[UNITS[s - 1]] * (1 + 1) // 2)
+                scalar_sums(s - 1, 1)
             project(s, have(s, [0, 1, 2, 3]))
             transpose(s + 2, have(s + 2, [0, 1, 2, 3]))
             if have(s, [0, 1]):

@@ -23,8 +23,8 @@ STATS = 3
 
 UNITS = [4, 4] + [8] * 14 + [4, 2, 2]
 LOAD_AHEAD = 6
-SCALAR_PAIRS = {2: 2, 4: 4, 8: 7}
-GPSIMD_SCALES = {2: 1, 4: 3, 8: 6}
+SCALAR_PAIRS = [4, 4] + [8, 9] * 7 + [4, 2, 2]
+GPSIMD_SCALES = [4, 4] + [6] * 14 + [3, 1, 1]
 VECTOR_SCALED = 4
 
 FLOPS = 2 * BATCH * TOKENS * K * OUT_COLS
@@ -134,10 +134,11 @@ def tile_ufoattention_pb_t_kernel(tc, queries, Wq, bq, gamma, out):
                 )
 
         def scalar_sums(r, half):
-            n, pairs = UNITS[r], SCALAR_PAIRS[UNITS[r]]
+            n, pairs = UNITS[r], SCALAR_PAIRS[r]
             if r not in sumsq_tiles:
                 sumsq_tiles[r] = small.tile([P, n * HEADS], F32, name="sumsq")
-                square_tiles[r] = sq_pool.tile([P, 2 * pairs, HEAD_DIM], F32, name="squares")
+                if pairs:
+                    square_tiles[r] = sq_pool.tile([P, 2 * pairs, HEAD_DIM], F32, name="squares")
             for j in range(2 * pairs * half // 2, 2 * pairs * (half + 1) // 2):
                 nc.scalar.activation(
                     out=square_tiles[r][:, j, :],
@@ -147,7 +148,7 @@ def tile_ufoattention_pb_t_kernel(tc, queries, Wq, bq, gamma, out):
                 )
 
         def vector_stats(r, part, parts_n):
-            n, first = UNITS[r], SCALAR_PAIRS[UNITS[r]]
+            n, first = UNITS[r], SCALAR_PAIRS[r]
             if r not in stats_tiles:
                 stats_tiles[r] = small.tile([P, 2 * n - first, 2 * STATS], F32, name="stats")
             count = 2 * n - first
@@ -167,7 +168,7 @@ def tile_ufoattention_pb_t_kernel(tc, queries, Wq, bq, gamma, out):
         def vector_sums(r):
             stats = stats_tiles[r][:].rearrange("p j (e c) -> p (j e) c", c=STATS)
             nc.vector.tensor_reduce(
-                out=sumsq_tiles[r][:, 2 * SCALAR_PAIRS[UNITS[r]] :],
+                out=sumsq_tiles[r][:, 2 * SCALAR_PAIRS[r] :],
                 in_=stats[:, :, 0:STATS:2],
                 axis=mybir.AxisListType.X,
                 op=ALU.add,
@@ -264,7 +265,7 @@ def tile_ufoattention_pb_t_kernel(tc, queries, Wq, bq, gamma, out):
             return 0 <= r < rounds
 
         warm = psum_t.tile([P, BANK_TILES, 2, P], F32, name="xt")
-        for i in range(5):
+        for i in range(3):
             nc.tensor.matmul(warm[:, i % 2, 0, :], lhsT=ident[:], rhs=ident[:], start=True, stop=True)
         transpose(0, have(0, [0, 1, 2, 3]))
         transpose(1, have(1, [0, 1, 2, 3]))
@@ -275,14 +276,14 @@ def tile_ufoattention_pb_t_kernel(tc, queries, Wq, bq, gamma, out):
             if live(s - 2) and s >= 4:
                 gains(s - 2)
                 vector_scaled = s - 2 >= rounds - VECTOR_SCALED
-                scaled = UNITS[s - 2] // 2 if vector_scaled else GPSIMD_SCALES[UNITS[s - 2]]
+                scaled = UNITS[s - 2] // 2 if vector_scaled else GPSIMD_SCALES[s - 2]
                 middle = (scaled + UNITS[s - 2] + 1) // 2
             if live(s):
                 quantise(s)
             if live(s - 2) and s < 4:
                 gains(s - 2)
                 vector_scaled = s - 2 >= rounds - VECTOR_SCALED
-                scaled = UNITS[s - 2] // 2 if vector_scaled else GPSIMD_SCALES[UNITS[s - 2]]
+                scaled = UNITS[s - 2] // 2 if vector_scaled else GPSIMD_SCALES[s - 2]
                 middle = (scaled + UNITS[s - 2] + 1) // 2
             if live(s - 2) and not vector_scaled:
                 scale_tiles_of(nc.gpsimd, s - 2, 0, scaled)

@@ -21,11 +21,11 @@ WORDS = K // 2
 BANK_TILES = 2
 STATS = 3
 
-UNITS = [4, 4] + [8] * 14 + [4, 2, 2]
+UNITS = [4, 4] + [8] * 15
 LOAD_AHEAD = 6
-SCALAR_PAIRS = [4, 4] + [8, 9] * 7 + [4, 2, 2]
-GPSIMD_SCALES = [4, 4] + [6] * 14 + [3, 1, 1]
-VECTOR_SCALED = 4
+SCALAR_PAIRS = [4, 4] + [8] * 14 + [6]
+GPSIMD_SCALES = [4, 4] + [6] * 15
+VECTOR_SCALED = 2
 
 FLOPS = 2 * BATCH * TOKENS * K * OUT_COLS
 
@@ -209,12 +209,32 @@ def tile_ufoattention_pb_t_kernel(tc, queries, Wq, bq, gamma, out):
                         scale=gain_tiles[r][:, i, h : h + 1],
                     )
 
-        def store(r):
+        def vector_scale_heads(r, first, last):
+            n = UNITS[r]
+            gain = gain_tiles[r][:, :, first:last].rearrange("p i h -> p h i")
+            nc.vector.tensor_tensor(
+                out=q_tiles[r][:, first:last, :, :],
+                in0=q_tiles[r][:, first:last, :, :],
+                in1=gain.unsqueeze(3).to_broadcast([P, last - first, n, HEAD_DIM]),
+                op=ALU.mult,
+            )
+
+        def scalar_scale_heads(r, first, last):
+            for h in range(first, last):
+                for i in range(UNITS[r]):
+                    nc.scalar.activation(
+                        out=q_tiles[r][:, h, i, :],
+                        in_=q_tiles[r][:, h, i, :],
+                        func=ACT.Copy,
+                        scale=gain_tiles[r][:, i, h : h + 1],
+                    )
+
+        def store(r, first=0, last=HEADS):
             n = UNITS[r]
             b, n0 = first_token[r] // TOKENS, first_token[r] % TOKENS
             nc.sync.dma_start(
-                out=out[b, :, n0 : n0 + n * P, :].rearrange("h (p i) d -> p h (i d)", i=n),
-                in_=q_tiles[r][:].rearrange("p h i d -> p h (i d)"),
+                out=out[b, first:last, n0 : n0 + n * P, :].rearrange("h (p i) d -> p h (i d)", i=n),
+                in_=q_tiles[r][:, first:last, :, :].rearrange("p h i d -> p h (i d)"),
             )
 
         load(0)
@@ -307,13 +327,19 @@ def tile_ufoattention_pb_t_kernel(tc, queries, Wq, bq, gamma, out):
                 vector_sums(s - 1)
             if have(s, [2, 3]):
                 add_bias(s, have(s, [2, 3]))
-            if live(s - 2) and vector_scaled:
-                scale_tiles_of(nc.vector, s - 2, 0, scaled)
-            if live(s - 2):
+            by_heads = s - 2 >= rounds - 2
+            if by_heads:
+                for h in (0, 2):
+                    (vector_scale_heads if h < 2 else scalar_scale_heads)(s - 2, h, h + 1)
+                    store(s - 2, h, h + 1)
+            elif live(s - 2):
                 scalar_scale(s - 2, scaled, middle)
             if live(s - 1):
                 reciprocal_norm(s - 1)
-            if live(s - 2):
+            if by_heads:
+                for h in (1, 3):
+                    (vector_scale_heads if h < 2 else scalar_scale_heads)(s - 2, h, h + 1)
+                    store(s - 2, h, h + 1)
+            elif live(s - 2):
                 scalar_scale(s - 2, middle, UNITS[s - 2])
-            if live(s - 2):
                 store(s - 2)

import math
from contextlib import ExitStack

import concourse.mybir as mybir
from concourse.masks import make_identity

F32 = mybir.dt.float32
BF16 = mybir.dt.bfloat16
U32 = mybir.dt.uint32
U8 = mybir.dt.uint8
FP8X4 = mybir.dt.float8_e4m3fn_x4
ACT = mybir.ActivationFunctionType
ALU = mybir.AluOpType

P = 128
BATCH, TOKENS, K = 4, 4096, 512
HEADS, HEAD_DIM = 4, 64
OUT_COLS = HEADS * HEAD_DIM
PACK = 4
WORDS = K // 2
BANK_TILES = 2
STATS = 3

UNITS = [4, 4] + [8] * 15
LOAD_AHEAD = 6
SCALAR_PAIRS = [4, 4] + [8] * 14 + [6]
GPSIMD_SCALES = [4, 4] + [6] * 15
VECTOR_SCALED = 2

FLOPS = 2 * BATCH * TOKENS * K * OUT_COLS


def tile_ufoattention_pb_t_kernel(tc, queries, Wq, bq, gamma, out):
    nc = tc.nc
    with ExitStack() as ctx:
        ctx.enter_context(tc.manual_schedule())
        const = ctx.enter_context(tc.tile_pool(name="const", bufs=1))
        x_pool = ctx.enter_context(tc.tile_pool(name="x", bufs=LOAD_AHEAD + 5))
        mx_pool = ctx.enter_context(tc.tile_pool(name="mx", bufs=2))
        q_pool = ctx.enter_context(tc.tile_pool(name="q", bufs=5))
        small = ctx.enter_context(tc.tile_pool(name="small", bufs=4))
        sq_pool = ctx.enter_context(tc.tile_pool(name="sq", bufs=3))
        psum_t = ctx.enter_context(tc.psum_pool(name="psum_t", bufs=4))
        psum_q = ctx.enter_context(tc.psum_pool(name="psum_q", bufs=4))

        x_rows = queries.flatten_outer_dims()
        first_token = [P * sum(UNITS[:r]) for r in range(len(UNITS))]
        rounds = len(UNITS)

        x_tiles, xt_banks, grouped_tiles, code_tiles, scale_tiles = {}, {}, {}, {}, {}
        acc_banks, q_tiles, stats_tiles, sumsq_tiles, rnorm_tiles, gain_tiles = {}, {}, {}, {}, {}, {}
        square_tiles = {}

        def load(r, pieces=1):
            n = UNITS[r]
            x_tiles[r] = x_pool.tile([P, n * K], BF16, name="x_sb")
            rows = x_rows[first_token[r] : first_token[r] + n * P, :].rearrange("(p i) k -> p (i k)", i=n)
            width = n * K // pieces
            for j in range(pieces):
                nc.sync.dma_start(
                    out=x_tiles[r][:, j * width : (j + 1) * width],
                    in_=rows[:, j * width : (j + 1) * width],
                )

        def transpose(r, banks):
            if not banks:
                return
            x_words = x_tiles[r][:].bitcast(F32)
            for bank in banks:
                xt = psum_t.tile([P, BANK_TILES, 2, P], F32, name="xt")
                for i in range(BANK_TILES):
                    first = (bank * BANK_TILES + i) * WORDS
                    for u in range(2):
                        nc.tensor.transpose(
                            xt[:, i, u, :], x_words[:, first + u : first + WORDS : 2], ident[:]
                        )
                xt_banks.setdefault(r, []).append(xt)

        def regroup(r, part, parts_n):
            n = UNITS[r]
            if r not in grouped_tiles:
                grouped_tiles[r] = mx_pool.tile([P, n * K], BF16, align_bytes=64, name="grouped")
            grouped_words = grouped_tiles[r][:].bitcast(F32)
            count = n // BANK_TILES
            for bank in range(count * part // parts_n, count * (part + 1) // parts_n):
                xt = xt_banks[r][bank]
                dst = grouped_words[
                    :, bank * BANK_TILES * WORDS : (bank + 1) * BANK_TILES * WORDS
                ].rearrange("p (i r u) -> p i r u", i=BANK_TILES, u=2)
                nc.scalar.copy(out=dst, in_=xt[:].rearrange("p i u r -> p i r u"))

        def quantise(r, first=0, last=None):
            n = UNITS[r]
            last = n if last is None else last
            if r not in code_tiles:
                code_tiles[r] = mx_pool.tile([P, n * P], U32, align_bytes=64, name="codes")
                scale_tiles[r] = mx_pool.tile([P, n * P], U8, align_bytes=64, name="scales")
            nc.vector.quantize_mx(
                out=code_tiles[r][:, first * P : last * P].bitcast(FP8X4),
                scales=scale_tiles[r][:, first * P : last * P],
                in_=grouped_tiles[r][:, first * K : last * K],
            )

        def project(r, banks):
            if not banks:
                return
            codes, scales = code_tiles[r], scale_tiles[r]
            for bank in banks:
                acc = psum_q.tile([P, BANK_TILES, OUT_COLS], F32, name="acc")
                for i in range(BANK_TILES):
                    cols = slice((bank * BANK_TILES + i) * P, (bank * BANK_TILES + i + 1) * P)
                    nc.tensor.matmul_mx(
                        out=acc[:, i, :],
                        lhsT=codes[:, cols].bitcast(FP8X4),
                        lhsT_scale=scales[:, cols],
                        rhs=w_codes[:].bitcast(FP8X4),
                        rhs_scale=w_scales[:],
                        start=True,
                        stop=True,
                    )
                acc_banks.setdefault(r, []).append(acc)

        def add_bias(r, banks):
            n = UNITS[r]
            if r not in q_tiles:
                q_tiles[r] = q_pool.tile([P, HEADS, n, HEAD_DIM], F32, name="q_sb")
            for bank in banks:
                acc = acc_banks[r][bank]
                nc.vector.tensor_tensor(
                    out=q_tiles[r][:, :, bank * BANK_TILES : (bank + 1) * BANK_TILES, :],
                    in0=acc[:].rearrange("p i (h d) -> p h i d", h=HEADS),
                    in1=bias_bank[:],
                    op=ALU.add,
                )

        def scalar_sums(r, half):
            n, pairs = UNITS[r], SCALAR_PAIRS[r]
            if r not in sumsq_tiles:
                sumsq_tiles[r] = small.tile([P, n * HEADS], F32, name="sumsq")
                if pairs:
                    square_tiles[r] = sq_pool.tile([P, 2 * pairs, HEAD_DIM], F32, name="squares")
            for j in range(2 * pairs * half // 2, 2 * pairs * (half + 1) // 2):
                nc.scalar.activation(
                    out=square_tiles[r][:, j, :],
                    in_=q_tiles[r][:, j % HEADS, j // HEADS, :],
                    func=ACT.Square,
                    accum_out=sumsq_tiles[r][:, j : j + 1],
                )

        def vector_stats(r, part, parts_n):
            n, first = UNITS[r], SCALAR_PAIRS[r]
            if r not in stats_tiles:
                stats_tiles[r] = small.tile([P, 2 * n - first, 2 * STATS], F32, name="stats")
            count = 2 * n - first
            for j in range(first + count * part // parts_n, first + count * (part + 1) // parts_n):
                i, h = j // 2, 2 * (j % 2)
                nc.vector.bn_stats(
                    out=stats_tiles[r][:, j - first, :],
                    in_=q_tiles[r][:, h : h + 2, i, :].rearrange("p h d -> p d h"),
                )

        def mean_squares(r):
            stats = stats_tiles[r][:].rearrange("p j (e c) -> p (j e) c", c=STATS)
            nc.scalar.activation(
                out=stats[:, :, 0], in_=stats[:, :, 1], func=ACT.Square, scale=math.sqrt(HEAD_DIM)
            )

        def vector_sums(r):
            stats = stats_tiles[r][:].rearrange("p j (e c) -> p (j e) c", c=STATS)
            nc.vector.tensor_reduce(
                out=sumsq_tiles[r][:, 2 * SCALAR_PAIRS[r] :],
                in_=stats[:, :, 0:STATS:2],
                axis=mybir.AxisListType.X,
                op=ALU.add,
            )

        def reciprocal_norm(r):
            rnorm_tiles[r] = small.tile([P, UNITS[r] * HEADS], F32, name="rnorm")
            nc.scalar.activation(
                out=rnorm_tiles[r][:], in_=sumsq_tiles[r][:], func=ACT.Abs_reciprocal_sqrt
            )

        def gains(r):
            n = UNITS[r]
            gain_tiles[r] = small.tile([P, n, HEADS], F32, name="gain")
            nc.vector.tensor_tensor(
                out=gain_tiles[r][:],
                in0=rnorm_tiles[r][:].rearrange("p (i h) -> p i h", h=HEADS),
                in1=gamma_sb[:].unsqueeze(1).to_broadcast([P, n, HEADS]),
                op=ALU.mult,
            )

        def scale_tiles_of(engine, r, first, last):
            gain = gain_tiles[r][:, first:last, :].rearrange("p i h -> p h i")
            engine.tensor_tensor(
                out=q_tiles[r][:, :, first:last, :],
                in0=q_tiles[r][:, :, first:last, :],
                in1=gain.unsqueeze(3).to_broadcast([P, HEADS, last - first, HEAD_DIM]),
                op=ALU.mult,
            )

        def scalar_scale(r, first, last):
            for i in range(first, last):
                for h in range(HEADS):
                    nc.scalar.activation(
                        out=q_tiles[r][:, h, i, :],
                        in_=q_tiles[r][:, h, i, :],
                        func=ACT.Copy,
                        scale=gain_tiles[r][:, i, h : h + 1],
                    )

        def vector_scale_heads(r, first, last):
            n = UNITS[r]
            gain = gain_tiles[r][:, :, first:last].rearrange("p i h -> p h i")
            nc.vector.tensor_tensor(
                out=q_tiles[r][:, first:last, :, :],
                in0=q_tiles[r][:, first:last, :, :],
                in1=gain.unsqueeze(3).to_broadcast([P, last - first, n, HEAD_DIM]),
                op=ALU.mult,
            )

        def scalar_scale_heads(r, first, last):
            for h in range(first, last):
                for i in range(UNITS[r]):
                    nc.scalar.activation(
                        out=q_tiles[r][:, h, i, :],
                        in_=q_tiles[r][:, h, i, :],
                        func=ACT.Copy,
                        scale=gain_tiles[r][:, i, h : h + 1],
                    )

        def store(r, first=0, last=HEADS):
            n = UNITS[r]
            b, n0 = first_token[r] // TOKENS, first_token[r] % TOKENS
            nc.sync.dma_start(
                out=out[b, first:last, n0 : n0 + n * P, :].rearrange("h (p i) d -> p h (i d)", i=n),
                in_=q_tiles[r][:, first:last, :, :].rearrange("p h i d -> p h (i d)"),
            )

        load(0)
        load(1)
        ident = const.tile([P, P], F32)
        make_identity(nc, ident[:])

        w_raw = const.tile([P, PACK, OUT_COLS], BF16)
        nc.scalar.dma_start(out=w_raw[:], in_=Wq.rearrange("(p t) c -> p t c", t=PACK))
        bias_bf = const.tile([P, OUT_COLS], BF16)
        nc.scalar.dma_start(out=bias_bf[:], in_=bq.partition_broadcast(P))
        gamma_bf = const.tile([P, HEADS], BF16)
        nc.scalar.dma_start(
            out=gamma_bf[:],
            in_=gamma.rearrange("a h b c -> (a h b c)").partition_broadcast(P),
        )
        for r in range(2, LOAD_AHEAD + 2):
            load(r)

        one = const.tile([P, 1], F32)
        nc.vector.memset(one[:], 1.0)
        nc.scalar.activation(out=one[:], in_=one[:], func=ACT.Abs_reciprocal_sqrt)

        w_grouped = const.tile([P, OUT_COLS, PACK], BF16, align_bytes=64)
        nc.vector.tensor_copy(out=w_grouped[:], in_=w_raw[:].rearrange("p t c -> p c t"))
        w_codes = const.tile([P, OUT_COLS], U32, align_bytes=64)
        w_scales = const.tile([P, OUT_COLS], U8, align_bytes=64)
        nc.vector.quantize_mx(
            out=w_codes[:].bitcast(FP8X4),
            scales=w_scales[:],
            in_=w_grouped[:].rearrange("p c t -> p (c t)"),
        )
        bias_bank = const.tile([P, HEADS, BANK_TILES, HEAD_DIM], F32)
        gamma_sb = const.tile([P, HEADS], F32)

        def bias_and_gains():
            for i in range(BANK_TILES):
                nc.vector.tensor_copy(
                    out=bias_bank[:, :, i, :],
                    in_=bias_bf[:].rearrange("p (h d) -> p h d", h=HEADS),
                )
            nc.vector.tensor_copy(out=gamma_sb[:], in_=gamma_bf[:])

        def have(r, banks):
            return [b for b in banks if 0 <= r < rounds and b < UNITS[r] // BANK_TILES]

        def live(r):
            return 0 <= r < rounds

        warm = psum_t.tile([P, BANK_TILES, 2, P], F32, name="xt")
        for i in range(3):
            nc.tensor.matmul(warm[:, i % 2, 0, :], lhsT=ident[:], rhs=ident[:], start=True, stop=True)
        transpose(0, have(0, [0, 1, 2, 3]))
        transpose(1, have(1, [0, 1, 2, 3]))
        regroup(0, 0, 1)
        for s in range(rounds + 2):
            if live(s + 2 + LOAD_AHEAD):
                load(s + 2 + LOAD_AHEAD)
            if live(s - 2) and s >= 4:
                gains(s - 2)
                vector_scaled = s - 2 >= rounds - VECTOR_SCALED
                scaled = UNITS[s - 2] // 2 if vector_scaled else GPSIMD_SCALES[s - 2]
                middle = (scaled + UNITS[s - 2] + 1) // 2
            if live(s):
                quantise(s)
            if live(s - 2) and s < 4:
                gains(s - 2)
                vector_scaled = s - 2 >= rounds - VECTOR_SCALED
                scaled = UNITS[s - 2] // 2 if vector_scaled else GPSIMD_SCALES[s - 2]
                middle = (scaled + UNITS[s - 2] + 1) // 2
            if live(s - 2) and not vector_scaled:
                scale_tiles_of(nc.gpsimd, s - 2, 0, scaled)
            if live(s + 1):
                regroup(s + 1, 0, 1)
            if s == 0:
                bias_and_gains()
            if live(s - 1):
                vector_stats(s - 1, 0, 1)
            if live(s - 1):
                scalar_sums(s - 1, 0)
            if live(s - 1):
                mean_squares(s - 1)
            if live(s - 1):
                scalar_sums(s - 1, 1)
            project(s, have(s, [0, 1, 2, 3]))
            transpose(s + 2, have(s + 2, [0, 1, 2, 3]))
            if have(s, [0, 1]):
                add_bias(s, have(s, [0, 1]))
            if live(s - 1):
                vector_sums(s - 1)
            if have(s, [2, 3]):
                add_bias(s, have(s, [2, 3]))
            by_heads = s - 2 >= rounds - 2
            if by_heads:
                for h in (0, 2):
                    (vector_scale_heads if h < 2 else scalar_scale_heads)(s - 2, h, h + 1)
                    store(s - 2, h, h + 1)
            elif live(s - 2):
                scalar_scale(s - 2, scaled, middle)
            if live(s - 1):
                reciprocal_norm(s - 1)
            if by_heads:
                for h in (1, 3):
                    (vector_scale_heads if h < 2 else scalar_scale_heads)(s - 2, h, h + 1)
                    store(s - 2, h, h + 1)
            elif live(s - 2):
                scalar_scale(s - 2, middle, UNITS[s - 2])
                store(s - 2)
